import numpy as np
import ml_dtypes

BF16 = ml_dtypes.bfloat16


def bf(x):
    return np.asarray(x, np.float32).astype(BF16)


def f32(x):
    return np.asarray(x, np.float32)


def f64(x):
    return np.asarray(x).astype(np.float64)


def striped(idx):
    return np.tile(idx.reshape(-1, 16).T, (8, 1))


H, D, HALF, S, N, MEM = 4, 128, 64, 2048, 512, 3
ROPE_BASE = 10000.0


def setup_inputs():
    inv_freq = ROPE_BASE ** (-np.arange(HALF) / HALF)
    phase = np.random.uniform(0.0, 2.0 * np.pi, (HALF, 1))
    freqs = inv_freq[:, None] * np.arange(S)[None, :] + phase
    emb = np.concatenate([freqs, freqs], axis=0)
    trig = np.concatenate([np.cos(emb), np.sin(emb)], axis=0)
    return {"mem_keys": f32(np.random.standard_normal((H * D, MEM * N))), "k_new": f32(np.random.standard_normal((H * D, N))), "trig": f32(trig), "offs": striped(np.random.permutation(np.tile(np.arange(S), 2))[:N])}


def reference(mem_keys, k_new, trig, offs):
    idx = offs[:16].T.reshape(-1)
    cos = f64(trig)[:D, idx]
    sin = f64(trig)[D:, idx]
    kk = f64(k_new).reshape(H, D, N)
    rot = np.concatenate([-kk[:, HALF:], kk[:, :HALF]], axis=1)
    fresh = (kk * cos[None] + rot * sin[None]).reshape(H * D, N)
    return np.concatenate([f64(mem_keys)[:, N:], fresh], axis=1)

@@ -1,0 +1,56 @@
+import concourse.mybir as mybir
+
+H, D, HALF, S, N, MEM = 4, 128, 64, 2048, 512, 3
+KEPT = (MEM - 1) * N
+F32, U16 = mybir.dt.float32, mybir.dt.uint16
+MULT, ADD = mybir.AluOpType.mult, mybir.AluOpType.add
+
+BYTES = 4 * (2 * H * D * KEPT + 2 * H * D * N + 2 * D * S) + 2 * D * (N // 16)
+
+
+def tile_externalmemory_kernel(tc, mem_keys, k_new, trig, offs, out):
+    nc = tc.nc
+    with tc.tile_pool(name="held", bufs=1) as held:
+        offsets = held.tile([D, N // 16], U16, name="offsets")
+        nc.sync.dma_start(offsets[:], offs)
+        cos = held.tile([D, S], F32, name="cos")
+        nc.sync.dma_start(cos[:], trig[0:D, :])
+
+        keys = []
+        for h in range(H):
+            k_h = held.tile([D, N], F32, name=f"k{h}")
+            nc.sync.dma_start(k_h[:], k_new[h * D : (h + 1) * D, :])
+            keys.append(k_h)
+
+        sin = held.tile([D, S], F32, name="sin")
+        nc.sync.dma_start(sin[:], trig[D : 2 * D, :])
+
+        rots = []
+        for h in range(H):
+            rot_h = held.tile([D, N], F32, name=f"rot{h}")
+            nc.sync.dma_start(rot_h[0:HALF, :], k_new[h * D + HALF : (h + 1) * D, :])
+            nc.sync.dma_start(rot_h[HALF:D, :], k_new[h * D : h * D + HALF, :])
+            rots.append(rot_h)
+
+        kept = []
+        for h in range(H):
+            kept_h = held.tile([D, KEPT], F32, name=f"kept{h}")
+            nc.sync.dma_start(kept_h[:], mem_keys[h * D : (h + 1) * D, N : MEM * N])
+            kept.append(kept_h)
+
+        for h in range(H):
+            nc.sync.dma_start(out[h * D : (h + 1) * D, 0:KEPT], kept[h][:])
+
+        with_cos = []
+        for h in range(H):
+            a_h = held.tile([D, N], F32, name=f"a{h}")
+            nc.vector.tensor_tensor(a_h[:], cos[:].indirect(offsets[:]), keys[h][:], MULT)
+            with_cos.append(a_h)
+
+        for h in range(H):
+            nc.scalar.mul(rots[h][0:HALF, :], rots[h][0:HALF, :], -1.0)
+            b_h = held.tile([D, N], F32, name=f"b{h}")
+            nc.vector.tensor_tensor(b_h[:], sin[:].indirect(offsets[:]), rots[h][:], MULT)
+            fresh_h = held.tile([D, N], F32, name=f"fresh{h}")
+            nc.vector.tensor_tensor(fresh_h[:], with_cos[h][:], b_h[:], ADD)
+            nc.scalar.dma_start(out[h * D : (h + 1) * D, KEPT : KEPT + N], fresh_h[:])

@@ -1,16 +1,22 @@
+import concourse.masks as masks
 import concourse.mybir as mybir
 
 H, D, HALF, S, N, MEM = 4, 128, 64, 2048, 512, 3
 KEPT = (MEM - 1) * N
 F32, U16 = mybir.dt.float32, mybir.dt.uint16
-MULT, ADD = mybir.AluOpType.mult, mybir.AluOpType.add
+MULT = mybir.AluOpType.mult
+NOT_EQUAL = mybir.AluOpType.not_equal
 
+FLOPS = 3 * H * D * N
 BYTES = 4 * (2 * H * D * KEPT + 2 * H * D * N + 2 * D * S) + 2 * D * (N // 16)
 
 
 def tile_externalmemory_kernel(tc, mem_keys, k_new, trig, offs, out):
     nc = tc.nc
-    with tc.tile_pool(name="held", bufs=1) as held:
+    with (
+        tc.tile_pool(name="held", bufs=1) as held,
+        tc.psum_pool(name="psum", bufs=1) as psum,
+    ):
         offsets = held.tile([D, N // 16], U16, name="offsets")
         nc.sync.dma_start(offsets[:], offs)
         cos = held.tile([D, S], F32, name="cos")
@@ -22,15 +28,9 @@ def tile_externalmemory_kernel(tc, mem_keys, k_new, trig, offs, out):
             nc.sync.dma_start(k_h[:], k_new[h * D : (h + 1) * D, :])
             keys.append(k_h)
 
-        sin = held.tile([D, S], F32, name="sin")
-        nc.sync.dma_start(sin[:], trig[D : 2 * D, :])
-
-        rots = []
-        for h in range(H):
-            rot_h = held.tile([D, N], F32, name=f"rot{h}")
-            nc.sync.dma_start(rot_h[0:HALF, :], k_new[h * D + HALF : (h + 1) * D, :])
-            nc.sync.dma_start(rot_h[HALF:D, :], k_new[h * D : h * D + HALF, :])
-            rots.append(rot_h)
+        sin_turned = held.tile([D, S], F32, name="sin_turned")
+        nc.sync.dma_start(sin_turned[0:HALF, :], trig[D + HALF : 2 * D, :])
+        nc.sync.dma_start(sin_turned[HALF:D, :], trig[D : D + HALF, :])
 
         kept = []
         for h in range(H):
@@ -41,16 +41,28 @@ def tile_externalmemory_kernel(tc, mem_keys, k_new, trig, offs, out):
         for h in range(H):
             nc.sync.dma_start(out[h * D : (h + 1) * D, 0:KEPT], kept[h][:])
 
-        with_cos = []
+        ident = held.tile([D, D], F32, name="ident")
+        masks.make_identity(nc, ident[:])
+        turn = held.tile([D, D], F32, name="turn")
+        nc.gpsimd.memset(turn[:], 0.0)
+        for base, fill in ((-HALF, -1.0), (HALF, 1.0)):
+            nc.gpsimd.affine_select(
+                out=turn[:], in_=turn[:], pattern=[[-1, D]], compare_op=NOT_EQUAL,
+                fill=fill, base=base, channel_multiplier=1,
+            )
+
+        banks = []
         for h in range(H):
             a_h = held.tile([D, N], F32, name=f"a{h}")
             nc.vector.tensor_tensor(a_h[:], cos[:].indirect(offsets[:]), keys[h][:], MULT)
-            with_cos.append(a_h)
+            bank_h = psum.tile([D, N], F32, name=f"bank{h}")
+            nc.tensor.matmul(bank_h[:], ident[:], a_h[:], start=True, stop=False)
+            banks.append(bank_h)
 
         for h in range(H):
-            nc.scalar.mul(rots[h][0:HALF, :], rots[h][0:HALF, :], -1.0)
-            b_h = held.tile([D, N], F32, name=f"b{h}")
-            nc.vector.tensor_tensor(b_h[:], sin[:].indirect(offsets[:]), rots[h][:], MULT)
+            c_h = held.tile([D, N], F32, name=f"c{h}")
+            nc.vector.tensor_tensor(c_h[:], sin_turned[:].indirect(offsets[:]), keys[h][:], MULT)
+            nc.tensor.matmul(banks[h][:], turn[:], c_h[:], start=False, stop=True)
             fresh_h = held.tile([D, N], F32, name=f"fresh{h}")
-            nc.vector.tensor_tensor(fresh_h[:], with_cos[h][:], b_h[:], ADD)
+            nc.scalar.copy(fresh_h[:], banks[h][:])
             nc.scalar.dma_start(out[h * D : (h + 1) * D, KEPT : KEPT + N], fresh_h[:])

@@ -1,10 +1,9 @@
-import concourse.masks as masks
 import concourse.mybir as mybir
 
 H, D, HALF, S, N, MEM = 4, 128, 64, 2048, 512, 3
 KEPT = (MEM - 1) * N
 F32, U16 = mybir.dt.float32, mybir.dt.uint16
-MULT = mybir.AluOpType.mult
+MULT, ADD = mybir.AluOpType.mult, mybir.AluOpType.add
 NOT_EQUAL = mybir.AluOpType.not_equal
 
 FLOPS = 3 * H * D * N
@@ -28,9 +27,8 @@ def tile_externalmemory_kernel(tc, mem_keys, k_new, trig, offs, out):
             nc.sync.dma_start(k_h[:], k_new[h * D : (h + 1) * D, :])
             keys.append(k_h)
 
-        sin_turned = held.tile([D, S], F32, name="sin_turned")
-        nc.sync.dma_start(sin_turned[0:HALF, :], trig[D + HALF : 2 * D, :])
-        nc.sync.dma_start(sin_turned[HALF:D, :], trig[D : D + HALF, :])
+        sin = held.tile([D, S], F32, name="sin")
+        nc.sync.dma_start(sin[:], trig[D : 2 * D, :])
 
         kept = []
         for h in range(H):
@@ -41,8 +39,6 @@ def tile_externalmemory_kernel(tc, mem_keys, k_new, trig, offs, out):
         for h in range(H):
             nc.sync.dma_start(out[h * D : (h + 1) * D, 0:KEPT], kept[h][:])
 
-        ident = held.tile([D, D], F32, name="ident")
-        masks.make_identity(nc, ident[:])
         turn = held.tile([D, D], F32, name="turn")
         nc.gpsimd.memset(turn[:], 0.0)
         for base, fill in ((-HALF, -1.0), (HALF, 1.0)):
@@ -51,18 +47,23 @@ def tile_externalmemory_kernel(tc, mem_keys, k_new, trig, offs, out):
                 fill=fill, base=base, channel_multiplier=1,
             )
 
-        banks = []
+        rots = []
+        for h in range(H):
+            bank_h = psum.tile([D, N], F32, name=f"bank{h}")
+            nc.tensor.matmul(bank_h[:], turn[:], keys[h][:], start=True, stop=True)
+            rot_h = held.tile([D, N], F32, name=f"rot{h}")
+            nc.scalar.copy(rot_h[:], bank_h[:])
+            rots.append(rot_h)
+
+        with_cos = []
         for h in range(H):
             a_h = held.tile([D, N], F32, name=f"a{h}")
             nc.vector.tensor_tensor(a_h[:], cos[:].indirect(offsets[:]), keys[h][:], MULT)
-            bank_h = psum.tile([D, N], F32, name=f"bank{h}")
-            nc.tensor.matmul(bank_h[:], ident[:], a_h[:], start=True, stop=False)
-            banks.append(bank_h)
+            with_cos.append(a_h)
 
         for h in range(H):
-            c_h = held.tile([D, N], F32, name=f"c{h}")
-            nc.vector.tensor_tensor(c_h[:], sin_turned[:].indirect(offsets[:]), keys[h][:], MULT)
-            nc.tensor.matmul(banks[h][:], turn[:], c_h[:], start=False, stop=True)
+            b_h = held.tile([D, N], F32, name=f"b{h}")
+            nc.vector.tensor_tensor(b_h[:], sin[:].indirect(offsets[:]), rots[h][:], MULT)
             fresh_h = held.tile([D, N], F32, name=f"fresh{h}")
-            nc.scalar.copy(fresh_h[:], banks[h][:])
+            nc.vector.tensor_tensor(fresh_h[:], with_cos[h][:], b_h[:], ADD)
             nc.scalar.dma_start(out[h * D : (h + 1) * D, KEPT : KEPT + N], fresh_h[:])

@@ -30,14 +30,11 @@ def tile_externalmemory_kernel(tc, mem_keys, k_new, trig, offs, out):
         sin = held.tile([D, S], F32, name="sin")
         nc.sync.dma_start(sin[:], trig[D : 2 * D, :])
 
-        kept = []
+        rows = []
         for h in range(H):
-            kept_h = held.tile([D, KEPT], F32, name=f"kept{h}")
-            nc.sync.dma_start(kept_h[:], mem_keys[h * D : (h + 1) * D, N : MEM * N])
-            kept.append(kept_h)
-
-        for h in range(H):
-            nc.sync.dma_start(out[h * D : (h + 1) * D, 0:KEPT], kept[h][:])
+            rows_h = held.tile([D, MEM * N], F32, name=f"rows{h}")
+            nc.sync.dma_start(rows_h[:, 0:KEPT], mem_keys[h * D : (h + 1) * D, N : MEM * N])
+            rows.append(rows_h)
 
         turn = held.tile([D, D], F32, name="turn")
         nc.gpsimd.memset(turn[:], 0.0)
@@ -64,6 +61,5 @@ def tile_externalmemory_kernel(tc, mem_keys, k_new, trig, offs, out):
         for h in range(H):
             b_h = held.tile([D, N], F32, name=f"b{h}")
             nc.vector.tensor_tensor(b_h[:], sin[:].indirect(offsets[:]), rots[h][:], MULT)
-            fresh_h = held.tile([D, N], F32, name=f"fresh{h}")
-            nc.vector.tensor_tensor(fresh_h[:], with_cos[h][:], b_h[:], ADD)
-            nc.scalar.dma_start(out[h * D : (h + 1) * D, KEPT : KEPT + N], fresh_h[:])
+            nc.vector.tensor_tensor(rows[h][:, KEPT : MEM * N], with_cos[h][:], b_h[:], ADD)
+            nc.scalar.dma_start(out[h * D : (h + 1) * D, :], rows[h][:])

@@ -30,11 +30,13 @@ def tile_externalmemory_kernel(tc, mem_keys, k_new, trig, offs, out):
         sin = held.tile([D, S], F32, name="sin")
         nc.sync.dma_start(sin[:], trig[D : 2 * D, :])
 
-        rows = []
-        for h in range(H):
-            rows_h = held.tile([D, MEM * N], F32, name=f"rows{h}")
-            nc.sync.dma_start(rows_h[:, 0:KEPT], mem_keys[h * D : (h + 1) * D, N : MEM * N])
-            rows.append(rows_h)
+        mem_by_head = mem_keys.rearrange("(h d) t -> d h t", d=D)
+        out_by_head = out.rearrange("(h d) t -> d h t", d=D)
+        kept = held.tile([D, H, KEPT], F32, name="kept")
+        for h in range(0, H, 2):
+            nc.sync.dma_start(kept[:, h : h + 2, :], mem_by_head[:, h : h + 2, N : MEM * N])
+        for h in range(0, H, 2):
+            nc.sync.dma_start(out_by_head[:, h : h + 2, 0:KEPT], kept[:, h : h + 2, :])
 
         turn = held.tile([D, D], F32, name="turn")
         nc.gpsimd.memset(turn[:], 0.0)
@@ -61,5 +63,6 @@ def tile_externalmemory_kernel(tc, mem_keys, k_new, trig, offs, out):
         for h in range(H):
             b_h = held.tile([D, N], F32, name=f"b{h}")
             nc.vector.tensor_tensor(b_h[:], sin[:].indirect(offsets[:]), rots[h][:], MULT)
-            nc.vector.tensor_tensor(rows[h][:, KEPT : MEM * N], with_cos[h][:], b_h[:], ADD)
-            nc.scalar.dma_start(out[h * D : (h + 1) * D, :], rows[h][:])
+            fresh_h = held.tile([D, N], F32, name=f"fresh{h}")
+            nc.vector.tensor_tensor(fresh_h[:], with_cos[h][:], b_h[:], ADD)
+            nc.scalar.dma_start(out[h * D : (h + 1) * D, KEPT : KEPT + N], fresh_h[:])

@@ -2,6 +2,8 @@ import concourse.mybir as mybir
 
 H, D, HALF, S, N, MEM = 4, 128, 64, 2048, 512, 3
 KEPT = (MEM - 1) * N
+ON_TENSOR = H // 2
+LAST_PIECES = 2
 F32, U16 = mybir.dt.float32, mybir.dt.uint16
 MULT, ADD = mybir.AluOpType.mult, mybir.AluOpType.add
 NOT_EQUAL = mybir.AluOpType.not_equal
@@ -18,15 +20,12 @@ def tile_externalmemory_kernel(tc, mem_keys, k_new, trig, offs, out):
     ):
         offsets = held.tile([D, N // 16], U16, name="offsets")
         nc.sync.dma_start(offsets[:], offs)
+        keys = [held.tile([D, N], F32, name=f"k{h}") for h in range(H)]
+        nc.sync.dma_start(keys[0][:], k_new[0:D, :])
         cos = held.tile([D, S], F32, name="cos")
         nc.sync.dma_start(cos[:], trig[0:D, :])
-
-        keys = []
-        for h in range(H):
-            k_h = held.tile([D, N], F32, name=f"k{h}")
-            nc.sync.dma_start(k_h[:], k_new[h * D : (h + 1) * D, :])
-            keys.append(k_h)
-
+        for h in range(1, H):
+            nc.sync.dma_start(keys[h][:], k_new[h * D : (h + 1) * D, :])
         sin = held.tile([D, S], F32, name="sin")
         nc.sync.dma_start(sin[:], trig[D : 2 * D, :])
 
@@ -45,6 +44,12 @@ def tile_externalmemory_kernel(tc, mem_keys, k_new, trig, offs, out):
                 out=turn[:], in_=turn[:], pattern=[[-1, D]], compare_op=NOT_EQUAL,
                 fill=fill, base=base, channel_multiplier=1,
             )
+        same = held.tile([D, D], F32, name="same")
+        nc.gpsimd.memset(same[:], 0.0)
+        nc.gpsimd.affine_select(
+            out=same[:], in_=same[:], pattern=[[-1, D]], compare_op=NOT_EQUAL,
+            fill=1.0, base=0, channel_multiplier=1,
+        )
 
         rots = []
         for h in range(H):
@@ -60,9 +65,26 @@ def tile_externalmemory_kernel(tc, mem_keys, k_new, trig, offs, out):
             nc.vector.tensor_tensor(a_h[:], cos[:].indirect(offsets[:]), keys[h][:], MULT)
             with_cos.append(a_h)
 
-        for h in range(H):
+        for h in range(ON_TENSOR):
             b_h = held.tile([D, N], F32, name=f"b{h}")
             nc.vector.tensor_tensor(b_h[:], sin[:].indirect(offsets[:]), rots[h][:], MULT)
+            sum_h = psum.tile([D, N], F32, name=f"sum{h}", tag=f"bank{H - 1}")
+            nc.tensor.matmul(sum_h[:], same[:], with_cos[h][:], start=True, stop=False)
+            nc.tensor.matmul(sum_h[:], same[:], b_h[:], start=False, stop=True)
             fresh_h = held.tile([D, N], F32, name=f"fresh{h}")
-            nc.vector.tensor_tensor(fresh_h[:], with_cos[h][:], b_h[:], ADD)
+            nc.scalar.copy(fresh_h[:], sum_h[:])
             nc.scalar.dma_start(out[h * D : (h + 1) * D, KEPT : KEPT + N], fresh_h[:])
+
+        for h in range(ON_TENSOR, H):
+            pieces = LAST_PIECES if h == H - 1 else 1
+            width = N // pieces
+            for p in range(pieces):
+                cols = slice(p * width, (p + 1) * width)
+                listed = offsets[:, p * width // 16 : (p + 1) * width // 16]
+                b_hp = held.tile([D, width], F32, name=f"b{h}_{p}")
+                nc.vector.tensor_tensor(b_hp[:], sin[:].indirect(listed), rots[h][:, cols], MULT)
+                fresh_hp = held.tile([D, width], F32, name=f"fresh{h}_{p}")
+                nc.vector.tensor_tensor(fresh_hp[:], with_cos[h][:, cols], b_hp[:], ADD)
+                nc.sync.dma_start(
+                    out[h * D : (h + 1) * D, KEPT + p * width : KEPT + (p + 1) * width], fresh_hp[:]
+                )

@@ -3,6 +3,7 @@ import concourse.mybir as mybir
 H, D, HALF, S, N, MEM = 4, 128, 64, 2048, 512, 3
 KEPT = (MEM - 1) * N
 ON_TENSOR = H // 2
+ROW = 256
 LAST_PIECES = 2
 F32, U16 = mybir.dt.float32, mybir.dt.uint16
 MULT, ADD = mybir.AluOpType.mult, mybir.AluOpType.add
@@ -20,18 +21,18 @@ def tile_externalmemory_kernel(tc, mem_keys, k_new, trig, offs, out):
     ):
         offsets = held.tile([D, N // 16], U16, name="offsets")
         nc.sync.dma_start(offsets[:], offs)
-        keys = [held.tile([D, N], F32, name=f"k{h}") for h in range(H)]
+        keys = [held.tile([D, N], F32, name=f"k{h}", align_bytes=ROW) for h in range(H)]
         nc.sync.dma_start(keys[0][:], k_new[0:D, :])
-        cos = held.tile([D, S], F32, name="cos")
+        cos = held.tile([D, S], F32, name="cos", align_bytes=ROW)
         nc.sync.dma_start(cos[:], trig[0:D, :])
         for h in range(1, H):
             nc.sync.dma_start(keys[h][:], k_new[h * D : (h + 1) * D, :])
-        sin = held.tile([D, S], F32, name="sin")
+        sin = held.tile([D, S], F32, name="sin", align_bytes=ROW)
         nc.sync.dma_start(sin[:], trig[D : 2 * D, :])
 
         mem_by_head = mem_keys.rearrange("(h d) t -> d h t", d=D)
         out_by_head = out.rearrange("(h d) t -> d h t", d=D)
-        kept = held.tile([D, H, KEPT], F32, name="kept")
+        kept = held.tile([D, H, KEPT], F32, name="kept", align_bytes=ROW)
         for h in range(0, H, 2):
             nc.sync.dma_start(kept[:, h : h + 2, :], mem_by_head[:, h : h + 2, N : MEM * N])
         for h in range(0, H, 2):
@@ -71,7 +72,7 @@ def tile_externalmemory_kernel(tc, mem_keys, k_new, trig, offs, out):
             sum_h = psum.tile([D, N], F32, name=f"sum{h}", tag=f"bank{H - 1}")
             nc.tensor.matmul(sum_h[:], same[:], with_cos[h][:], start=True, stop=False)
             nc.tensor.matmul(sum_h[:], same[:], b_h[:], start=False, stop=True)
-            fresh_h = held.tile([D, N], F32, name=f"fresh{h}")
+            fresh_h = held.tile([D, N], F32, name=f"fresh{h}", align_bytes=ROW)
             nc.scalar.copy(fresh_h[:], sum_h[:])
             nc.scalar.dma_start(out[h * D : (h + 1) * D, KEPT : KEPT + N], fresh_h[:])
 
@@ -83,7 +84,7 @@ def tile_externalmemory_kernel(tc, mem_keys, k_new, trig, offs, out):
                 listed = offsets[:, p * width // 16 : (p + 1) * width // 16]
                 b_hp = held.tile([D, width], F32, name=f"b{h}_{p}")
                 nc.vector.tensor_tensor(b_hp[:], sin[:].indirect(listed), rots[h][:, cols], MULT)
-                fresh_hp = held.tile([D, width], F32, name=f"fresh{h}_{p}")
+                fresh_hp = held.tile([D, width], F32, name=f"fresh{h}_{p}", align_bytes=ROW)
                 nc.vector.tensor_tensor(fresh_hp[:], with_cos[h][:, cols], b_hp[:], ADD)
                 nc.sync.dma_start(
                     out[h * D : (h + 1) * D, KEPT + p * width : KEPT + (p + 1) * width], fresh_hp[:]

@@ -2,9 +2,7 @@ import concourse.mybir as mybir
 
 H, D, HALF, S, N, MEM = 4, 128, 64, 2048, 512, 3
 KEPT = (MEM - 1) * N
-ON_TENSOR = H // 2
 ROW = 256
-LAST_PIECES = 2
 F32, U16 = mybir.dt.float32, mybir.dt.uint16
 MULT, ADD = mybir.AluOpType.mult, mybir.AluOpType.add
 NOT_EQUAL = mybir.AluOpType.not_equal
@@ -45,12 +43,6 @@ def tile_externalmemory_kernel(tc, mem_keys, k_new, trig, offs, out):
                 out=turn[:], in_=turn[:], pattern=[[-1, D]], compare_op=NOT_EQUAL,
                 fill=fill, base=base, channel_multiplier=1,
             )
-        same = held.tile([D, D], F32, name="same")
-        nc.gpsimd.memset(same[:], 0.0)
-        nc.gpsimd.affine_select(
-            out=same[:], in_=same[:], pattern=[[-1, D]], compare_op=NOT_EQUAL,
-            fill=1.0, base=0, channel_multiplier=1,
-        )
 
         rots = []
         for h in range(H):
@@ -66,26 +58,9 @@ def tile_externalmemory_kernel(tc, mem_keys, k_new, trig, offs, out):
             nc.vector.tensor_tensor(a_h[:], cos[:].indirect(offsets[:]), keys[h][:], MULT)
             with_cos.append(a_h)
 
-        for h in range(ON_TENSOR):
+        for h in range(H):
             b_h = held.tile([D, N], F32, name=f"b{h}")
             nc.vector.tensor_tensor(b_h[:], sin[:].indirect(offsets[:]), rots[h][:], MULT)
-            sum_h = psum.tile([D, N], F32, name=f"sum{h}", tag=f"bank{H - 1}")
-            nc.tensor.matmul(sum_h[:], same[:], with_cos[h][:], start=True, stop=False)
-            nc.tensor.matmul(sum_h[:], same[:], b_h[:], start=False, stop=True)
             fresh_h = held.tile([D, N], F32, name=f"fresh{h}", align_bytes=ROW)
-            nc.scalar.copy(fresh_h[:], sum_h[:])
-            nc.scalar.dma_start(out[h * D : (h + 1) * D, KEPT : KEPT + N], fresh_h[:])
-
-        for h in range(ON_TENSOR, H):
-            pieces = LAST_PIECES if h == H - 1 else 1
-            width = N // pieces
-            for p in range(pieces):
-                cols = slice(p * width, (p + 1) * width)
-                listed = offsets[:, p * width // 16 : (p + 1) * width // 16]
-                b_hp = held.tile([D, width], F32, name=f"b{h}_{p}")
-                nc.vector.tensor_tensor(b_hp[:], sin[:].indirect(listed), rots[h][:, cols], MULT)
-                fresh_hp = held.tile([D, width], F32, name=f"fresh{h}_{p}", align_bytes=ROW)
-                nc.vector.tensor_tensor(fresh_hp[:], with_cos[h][:, cols], b_hp[:], ADD)
-                nc.sync.dma_start(
-                    out[h * D : (h + 1) * D, KEPT + p * width : KEPT + (p + 1) * width], fresh_hp[:]
-                )
+            nc.vector.tensor_tensor(fresh_h[:], with_cos[h][:], b_h[:], ADD)
+            nc.sync.dma_start(out[h * D : (h + 1) * D, KEPT : KEPT + N], fresh_h[:])

@@ -22,7 +22,7 @@ def tile_externalmemory_kernel(tc, mem_keys, k_new, trig, offs, out):
         keys = [held.tile([D, N], F32, name=f"k{h}", align_bytes=ROW) for h in range(H)]
         nc.sync.dma_start(keys[0][:], k_new[0:D, :])
         cos = held.tile([D, S], F32, name="cos", align_bytes=ROW)
-        nc.sync.dma_start(cos[:], trig[0:D, :])
+        nc.scalar.dma_start(cos[:], trig[0:D, :])
         for h in range(1, H):
             nc.sync.dma_start(keys[h][:], k_new[h * D : (h + 1) * D, :])
         sin = held.tile([D, S], F32, name="sin", align_bytes=ROW)

@@ -28,13 +28,13 @@ def tile_externalmemory_kernel(tc, mem_keys, k_new, trig, offs, out):
         sin = held.tile([D, S], F32, name="sin", align_bytes=ROW)
         nc.sync.dma_start(sin[:], trig[D : 2 * D, :])
 
-        mem_by_head = mem_keys.rearrange("(h d) t -> d h t", d=D)
-        out_by_head = out.rearrange("(h d) t -> d h t", d=D)
+        mem_by_pair = mem_keys.rearrange("(i p two) t -> i p two t", p=D, two=2)
+        out_by_pair = out.rearrange("(i p two) t -> i p two t", p=D, two=2)
         kept = held.tile([D, H, KEPT], F32, name="kept", align_bytes=ROW)
-        for h in range(0, H, 2):
-            nc.sync.dma_start(kept[:, h : h + 2, :], mem_by_head[:, h : h + 2, N : MEM * N])
-        for h in range(0, H, 2):
-            nc.sync.dma_start(out_by_head[:, h : h + 2, 0:KEPT], kept[:, h : h + 2, :])
+        for i in range(H // 2):
+            nc.sync.dma_start(kept[:, 2 * i : 2 * i + 2, :], mem_by_pair[i, :, :, N : MEM * N])
+        for i in range(H // 2):
+            nc.sync.dma_start(out_by_pair[i, :, :, 0:KEPT], kept[:, 2 * i : 2 * i + 2, :])
 
         turn = held.tile([D, D], F32, name="turn")
         nc.gpsimd.memset(turn[:], 0.0)

import concourse.mybir as mybir

H, D, HALF, S, N, MEM = 4, 128, 64, 2048, 512, 3
KEPT = (MEM - 1) * N
ROW = 256
F32, U16 = mybir.dt.float32, mybir.dt.uint16
MULT, ADD = mybir.AluOpType.mult, mybir.AluOpType.add
NOT_EQUAL = mybir.AluOpType.not_equal

FLOPS = 3 * H * D * N
BYTES = 4 * (2 * H * D * KEPT + 2 * H * D * N + 2 * D * S) + 2 * D * (N // 16)


def tile_externalmemory_kernel(tc, mem_keys, k_new, trig, offs, out):
    nc = tc.nc
    with (
        tc.tile_pool(name="held", bufs=1) as held,
        tc.psum_pool(name="psum", bufs=1) as psum,
    ):
        offsets = held.tile([D, N // 16], U16, name="offsets")
        nc.sync.dma_start(offsets[:], offs)
        keys = [held.tile([D, N], F32, name=f"k{h}", align_bytes=ROW) for h in range(H)]
        nc.sync.dma_start(keys[0][:], k_new[0:D, :])
        cos = held.tile([D, S], F32, name="cos", align_bytes=ROW)
        nc.scalar.dma_start(cos[:], trig[0:D, :])
        for h in range(1, H):
            nc.sync.dma_start(keys[h][:], k_new[h * D : (h + 1) * D, :])
        sin = held.tile([D, S], F32, name="sin", align_bytes=ROW)
        nc.sync.dma_start(sin[:], trig[D : 2 * D, :])

        mem_by_pair = mem_keys.rearrange("(i p two) t -> i p two t", p=D, two=2)
        out_by_pair = out.rearrange("(i p two) t -> i p two t", p=D, two=2)
        kept = held.tile([D, H, KEPT], F32, name="kept", align_bytes=ROW)
        for i in range(H // 2):
            nc.sync.dma_start(kept[:, 2 * i : 2 * i + 2, :], mem_by_pair[i, :, :, N : MEM * N])
        for i in range(H // 2):
            nc.sync.dma_start(out_by_pair[i, :, :, 0:KEPT], kept[:, 2 * i : 2 * i + 2, :])

        turn = held.tile([D, D], F32, name="turn")
        nc.gpsimd.memset(turn[:], 0.0)
        for base, fill in ((-HALF, -1.0), (HALF, 1.0)):
            nc.gpsimd.affine_select(
                out=turn[:], in_=turn[:], pattern=[[-1, D]], compare_op=NOT_EQUAL,
                fill=fill, base=base, channel_multiplier=1,
            )

        rots = []
        for h in range(H):
            bank_h = psum.tile([D, N], F32, name=f"bank{h}")
            nc.tensor.matmul(bank_h[:], turn[:], keys[h][:], start=True, stop=True)
            rot_h = held.tile([D, N], F32, name=f"rot{h}")
            nc.scalar.copy(rot_h[:], bank_h[:])
            rots.append(rot_h)

        with_cos = []
        for h in range(H):
            a_h = held.tile([D, N], F32, name=f"a{h}")
            nc.vector.tensor_tensor(a_h[:], cos[:].indirect(offsets[:]), keys[h][:], MULT)
            with_cos.append(a_h)

        for h in range(H):
            b_h = held.tile([D, N], F32, name=f"b{h}")
            nc.vector.tensor_tensor(b_h[:], sin[:].indirect(offsets[:]), rots[h][:], MULT)
            fresh_h = held.tile([D, N], F32, name=f"fresh{h}", align_bytes=ROW)
            nc.vector.tensor_tensor(fresh_h[:], with_cos[h][:], b_h[:], ADD)
            nc.sync.dma_start(out[h * D : (h + 1) * D, KEPT : KEPT + N], fresh_h[:])
